import numpy as np
import ml_dtypes


def mxq(x, axis, fmt="e4m3"):
    dtype, down = {"e4m3": (ml_dtypes.float8_e4m3fn, 7), "e5m2": (ml_dtypes.float8_e5m2, 14)}[fmt]
    v = np.moveaxis(np.asarray(x, np.float32).astype(ml_dtypes.bfloat16).astype(np.float64), axis, -1)
    blocks = v.reshape(v.shape[:-1] + (-1, 32))
    amax = np.abs(blocks).max(-1, keepdims=True)
    byte = np.maximum(np.where(amax > 0, np.frexp(amax)[1] - 1 + 127, 0) - down, 1)
    scale = np.exp2(byte - 127.0)
    codes = (blocks / scale).astype(np.float32).astype(dtype).astype(np.float64)
    return np.moveaxis((codes * scale).reshape(v.shape), -1, axis)


WIDE = False


def mx_kscale(k):
    if not WIDE:
        return np.ones(k)
    levels = np.array([10, -10, 5, -5, 0])
    if k % 512:
        return np.exp2(np.random.permutation(np.resize(levels, k // 32))).repeat(32)
    a = np.empty((k // 512, 16))
    for p in range(k // 512):
        a[p, :8] = np.random.permutation(np.resize(levels, 8))
        for g in range(8):
            far = levels[np.abs(levels - a[p, g]) >= 10]
            a[p, g + 8] = far[np.random.randint(len(far))]
    return np.exp2(a.ravel()).repeat(32)


BF16 = ml_dtypes.bfloat16


def bf(x):
    return np.asarray(x, np.float32).astype(BF16)


def f64(x):
    return np.asarray(x).astype(np.float64)


N, L, D, M = 1024, 4, 1024, 1024


def l2norm(v):
    n = np.sqrt((v * v).sum(axis=-1, keepdims=True))
    return v / np.maximum(n, 1e-12)


def setup_inputs():
    s = mx_kscale(D)
    amp_f = 0.5 + 1.5 * np.random.random((N, L))[:, :, None]
    amp_v = 0.5 + 1.5 * np.random.random(N)[:, None]
    return {"feature": bf(np.random.standard_normal((N, L, D)) * amp_f * s),
            "aspect_v": bf(np.random.standard_normal((N, D)) * amp_v * s),
            "W": bf(np.random.standard_normal((M, D)) * np.sqrt(2.0 / (D + M)) / s),
            "b": bf(np.random.standard_normal(M) * 0.2)}


def reference(feature, aspect_v, W, b):
    wq = mxq(f64(W), 1, "e4m3")
    q = l2norm((mxq(f64(aspect_v), 1, "e4m3") @ wq.T) + f64(b))
    fn = l2norm((mxq(f64(feature), 2, "e4m3") @ wq.T) + f64(b))
    return q, fn.mean(axis=1)

@@ -1,0 +1,223 @@
+from contextlib import ExitStack
+
+import concourse.mybir as mybir
+from concourse.masks import make_identity
+
+F32 = mybir.dt.float32
+BF16 = mybir.dt.bfloat16
+U32 = mybir.dt.uint32
+U8 = mybir.dt.uint8
+FP8X4 = mybir.dt.float8_e4m3fn_x4
+ALU = mybir.AluOpType
+ACT = mybir.ActivationFunctionType
+
+P = 128
+SEGMENTS = 1024
+TOKENS = 4
+K = 1024
+M = 1024
+K_PASS = 4 * P
+PASSES = K // K_PASS
+WORDS = K // 2
+BANK = 512
+HALVES = M // BANK
+GROUPS = SEGMENTS // P
+TILES_PER_GROUP = 1 + TOKENS
+ROW_TILES = GROUPS * TILES_PER_GROUP
+W_TILES = M // P
+
+AHEAD_TRANSPOSE = 4
+AHEAD_QUANTISE = 2
+BEHIND_NORM = 1
+BEHIND_SCALE = 3
+BEHIND_MEAN = 4
+
+FLOPS = 2 * (SEGMENTS * TOKENS + SEGMENTS) * K * M
+
+
+def tile_linearattention_pa_kernel(tc, feature, aspect_v, W, b, out_0, out_1):
+    nc = tc.nc
+    with ExitStack() as stack:
+        const = stack.enter_context(tc.tile_pool(name="const", bufs=1))
+        raw_pool = stack.enter_context(tc.tile_pool(name="raw", bufs=GROUPS))
+        grouped_pool = stack.enter_context(tc.tile_pool(name="grouped", bufs=4))
+        mx_pool = stack.enter_context(tc.tile_pool(name="mx", bufs=4))
+        z_pool = stack.enter_context(tc.tile_pool(name="z", bufs=9))
+        scratch_pool = stack.enter_context(tc.tile_pool(name="scratch", bufs=2))
+        norm_pool = stack.enter_context(tc.tile_pool(name="norm", bufs=9))
+        out_pool = stack.enter_context(tc.tile_pool(name="out", bufs=2))
+        psum_t = stack.enter_context(tc.psum_pool(name="psum_t", bufs=2))
+        psum_y = stack.enter_context(tc.psum_pool(name="psum_y", bufs=6))
+
+        bias_row = const.tile([P, M], BF16)
+        nc.vector.memset(bias_row[:], 0.0)
+        ones = const.tile([P, P], BF16)
+        nc.vector.memset(ones[:], 1.0)
+        minus_half = const.tile([P, 1], F32)
+        nc.vector.memset(minus_half[:], -0.5)
+        identity = const.tile([P, P], F32)
+        make_identity(nc, identity[:])
+
+        w_raw = const.tile([P, W_TILES * K], BF16)
+        w_raw_tiles = w_raw[:].rearrange("p (t k) -> p t k", k=K)
+        w_rows = W.rearrange("(t p) k -> p t k", p=P)
+        raw = {}
+        for g in range(GROUPS):
+            raw[g] = raw_pool.tile([P, TILES_PER_GROUP * K], BF16, name="raw")
+
+        def load_w(t):
+            nc.sync.dma_start(out=w_raw_tiles[:, t : t + 2, :], in_=w_rows[:, t : t + 2, :])
+
+        def load_rows(i):
+            g, t = divmod(i, TILES_PER_GROUP)
+            segments = slice(g * P, (g + 1) * P)
+            rows = aspect_v[segments, :] if t == 0 else feature[segments, t - 1, :]
+            nc.sync.dma_start(out=raw[g][:, t * K : (t + 1) * K], in_=rows)
+
+        load_w(0)
+        nc.sync.dma_start(out=bias_row[0:1, :], in_=b.rearrange("(o m) -> o m", o=1))
+        load_w(2)
+        load_rows(0)
+        load_w(4)
+        load_w(6)
+        for i in range(1, ROW_TILES):
+            load_rows(i)
+
+        def transpose_rows(words, bank):
+            for c in range(PASSES):
+                for u in range(2):
+                    j = 2 * c + u
+                    nc.tensor.transpose(
+                        bank[:, j * P : (j + 1) * P],
+                        words[:, c * 2 * P + u : (c + 1) * 2 * P : 2],
+                        identity[:],
+                    )
+
+        def pairs_side_by_side(bank):
+            return bank.rearrange("p (c u r) -> p c r u", c=PASSES, u=2)
+
+        bias = const.tile([P, M], F32)
+        for h in range(HALVES):
+            half = slice(h * BANK, (h + 1) * BANK)
+            b_bank = psum_y.tile([P, BANK], F32, name="y")
+            nc.tensor.matmul(out=b_bank[:], lhsT=ones[:], rhs=bias_row[:, half], start=True, stop=True)
+            nc.vector.tensor_copy(out=bias[:, half], in_=b_bank[:])
+
+        w_grouped = const.tile([P, PASSES * M * 4], BF16, align_bytes=64)
+        w_grouped_words = w_grouped[:].bitcast(F32).rearrange(
+            "p (c m u) -> p c m u", c=PASSES, u=2
+        )
+        w_codes = const.tile([P, PASSES * M], U32, align_bytes=64)
+        w_scales = const.tile([P, PASSES * M], U8, align_bytes=64)
+        w_words = w_raw[:].bitcast(F32)
+        for t in range(W_TILES):
+            w_bank = psum_y.tile([P, BANK], F32, name="y")
+            transpose_rows(w_words[:, t * WORDS : (t + 1) * WORDS], w_bank)
+            target = w_grouped_words[:, :, t * P : (t + 1) * P, :]
+            if t % 2 == 0:
+                nc.scalar.copy(out=target, in_=pairs_side_by_side(w_bank))
+            else:
+                nc.vector.tensor_copy(out=target, in_=pairs_side_by_side(w_bank))
+            if (t + 1) % (BANK // P) == 0:
+                h = t // (BANK // P)
+                for c in range(PASSES):
+                    lo = c * M + h * BANK
+                    nc.vector.quantize_mx(
+                        out=w_codes[:, lo : lo + BANK].bitcast(FP8X4),
+                        scales=w_scales[:, lo : lo + BANK],
+                        in_=w_grouped[:, 4 * lo : 4 * (lo + BANK)],
+                    )
+
+        grouped = {}
+        codes = {}
+        scales = {}
+        z = {}
+        sumsq = {}
+        rnorm = {}
+        fm = {}
+
+        def transpose_and_regroup(i):
+            g, t = divmod(i, TILES_PER_GROUP)
+            x_bank = psum_t.tile([P, BANK], F32, name="xt")
+            transpose_rows(raw[g][:].bitcast(F32)[:, t * WORDS : (t + 1) * WORDS], x_bank)
+            grouped[i] = grouped_pool.tile([P, 2 * WORDS], BF16, name="grouped", align_bytes=64)
+            nc.scalar.copy(
+                out=grouped[i][:].bitcast(F32).rearrange("p (c r u) -> p c r u", c=PASSES, u=2),
+                in_=pairs_side_by_side(x_bank),
+            )
+
+        def quantise(i):
+            codes[i] = mx_pool.tile([P, PASSES * P], U32, name="codes", align_bytes=64)
+            scales[i] = mx_pool.tile([P, PASSES * P], U8, name="scales", align_bytes=64)
+            nc.vector.quantize_mx(
+                out=codes[i][:].bitcast(FP8X4), scales=scales[i][:], in_=grouped[i][:]
+            )
+
+        def multiply_and_add_bias(i):
+            z[i] = z_pool.tile([P, M], F32, name="z")
+            for h in range(HALVES):
+                y = psum_y.tile([P, BANK], F32, name="y")
+                for c in range(PASSES):
+                    rows = slice(c * P, (c + 1) * P)
+                    cols = slice(c * M + h * BANK, c * M + (h + 1) * BANK)
+                    nc.tensor.matmul_mx(
+                        out=y[:],
+                        lhsT=codes[i][:, rows].bitcast(FP8X4),
+                        lhsT_scale=scales[i][:, rows],
+                        rhs=w_codes[:, cols].bitcast(FP8X4),
+                        rhs_scale=w_scales[:, cols],
+                        start=(c == 0),
+                        stop=(c == PASSES - 1),
+                    )
+                half = slice(h * BANK, (h + 1) * BANK)
+                nc.vector.tensor_tensor(out=z[i][:, half], in0=y[:], in1=bias[:, half], op=ALU.add)
+
+        def sum_of_squares(i):
+            sumsq[i] = norm_pool.tile([P, 1], F32, name="sumsq")
+            squares = scratch_pool.tile([P, M], F32, name="squares")
+            nc.scalar.activation(out=squares[:], in_=z[i][:], func=ACT.Square, accum_out=sumsq[i][:])
+
+        def reciprocal_norm(i):
+            t = i % TILES_PER_GROUP
+            clamped = norm_pool.tile([P, 1], F32, name="clamped")
+            nc.gpsimd.tensor_scalar(
+                out=clamped[:], in0=sumsq[i][:], scalar1=1e-24,
+                scalar2=(1.0 if t == 0 else float(TOKENS * TOKENS)), op0=ALU.max, op1=ALU.mult,
+            )
+            rnorm[i] = norm_pool.tile([P, 1], F32, name="rnorm")
+            nc.gpsimd.tensor_tensor(out=rnorm[i][:], in0=clamped[:], in1=minus_half[:], op=ALU.pow)
+
+        def scale(i):
+            g, t = divmod(i, TILES_PER_GROUP)
+            if t == 0:
+                q = out_pool.tile([P, M], F32, name="q")
+                nc.scalar.activation(out=q[:], in_=z[i][:], func=ACT.Copy, scale=rnorm[i][:])
+                nc.sync.dma_start(out=out_0[g * P : (g + 1) * P, :], in_=q[:])
+            if t == 1:
+                fm[g] = out_pool.tile([P, M], F32, name="fm")
+                nc.scalar.activation(out=fm[g][:], in_=z[i][:], func=ACT.Copy, scale=rnorm[i][:])
+
+        def add_to_mean(i):
+            g, t = divmod(i, TILES_PER_GROUP)
+            if t >= 2:
+                nc.vector.scalar_tensor_tensor(
+                    out=fm[g][:], in0=z[i][:], scalar=rnorm[i][:], in1=fm[g][:],
+                    op0=ALU.mult, op1=ALU.add,
+                )
+            if t == TILES_PER_GROUP - 1:
+                nc.sync.dma_start(out=out_1[g * P : (g + 1) * P, :], in_=fm[g][:])
+
+        for step in range(-AHEAD_TRANSPOSE, ROW_TILES + BEHIND_MEAN):
+            if 0 <= step < ROW_TILES:
+                multiply_and_add_bias(step)
+            if step + AHEAD_TRANSPOSE < ROW_TILES:
+                transpose_and_regroup(step + AHEAD_TRANSPOSE)
+            if 0 <= step + AHEAD_QUANTISE < ROW_TILES:
+                quantise(step + AHEAD_QUANTISE)
+            if 0 <= step - BEHIND_NORM < ROW_TILES:
+                sum_of_squares(step - BEHIND_NORM)
+                reciprocal_norm(step - BEHIND_NORM)
+            if 0 <= step - BEHIND_SCALE < ROW_TILES:
+                scale(step - BEHIND_SCALE)
+            if 0 <= step - BEHIND_MEAN < ROW_TILES:
+                add_to_mean(step - BEHIND_MEAN)

@@ -22,10 +22,12 @@ WORDS = K // 2
 BANK = 512
 HALVES = M // BANK
 GROUPS = SEGMENTS // P
-TILES_PER_GROUP = 1 + TOKENS
+TILES_PER_GROUP = TOKENS + 1
+ASPECT = TOKENS
 ROW_TILES = GROUPS * TILES_PER_GROUP
 W_TILES = M // P
 
+EARLY = 2
 AHEAD_TRANSPOSE = 4
 AHEAD_QUANTISE = 2
 BEHIND_NORM = 1
@@ -71,16 +73,17 @@ def tile_linearattention_pa_kernel(tc, feature, aspect_v, W, b, out_0, out_1):
         def load_rows(i):
             g, t = divmod(i, TILES_PER_GROUP)
             segments = slice(g * P, (g + 1) * P)
-            rows = aspect_v[segments, :] if t == 0 else feature[segments, t - 1, :]
+            rows = aspect_v[segments, :] if t == ASPECT else feature[segments, t, :]
             nc.sync.dma_start(out=raw[g][:, t * K : (t + 1) * K], in_=rows)
 
         load_w(0)
-        nc.sync.dma_start(out=bias_row[0:1, :], in_=b.rearrange("(o m) -> o m", o=1))
         load_w(2)
         load_rows(0)
+        nc.sync.dma_start(out=bias_row[0:1, :], in_=b.rearrange("(o m) -> o m", o=1))
+        load_rows(1)
         load_w(4)
         load_w(6)
-        for i in range(1, ROW_TILES):
+        for i in range(EARLY, ROW_TILES):
             load_rows(i)
 
         def transpose_rows(words, bank):
@@ -96,12 +99,14 @@ def tile_linearattention_pa_kernel(tc, feature, aspect_v, W, b, out_0, out_1):
         def pairs_side_by_side(bank):
             return bank.rearrange("p (c u r) -> p c r u", c=PASSES, u=2)
 
-        bias = const.tile([P, M], F32)
-        for h in range(HALVES):
-            half = slice(h * BANK, (h + 1) * BANK)
-            b_bank = psum_y.tile([P, BANK], F32, name="y")
-            nc.tensor.matmul(out=b_bank[:], lhsT=ones[:], rhs=bias_row[:, half], start=True, stop=True)
-            nc.vector.tensor_copy(out=bias[:, half], in_=b_bank[:])
+        bias = const.tile([P, M], BF16)
+
+        def spread_bias():
+            b_bank = psum_y.tile([P, M], BF16, name="y")
+            for h in range(HALVES):
+                half = slice(h * BANK, (h + 1) * BANK)
+                nc.tensor.matmul(out=b_bank[:, half], lhsT=ones[:], rhs=bias_row[:, half], start=True, stop=True)
+            nc.scalar.copy(out=bias[:], in_=b_bank[:])
 
         w_grouped = const.tile([P, PASSES * M * 4], BF16, align_bytes=64)
         w_grouped_words = w_grouped[:].bitcast(F32).rearrange(
@@ -110,7 +115,8 @@ def tile_linearattention_pa_kernel(tc, feature, aspect_v, W, b, out_0, out_1):
         w_codes = const.tile([P, PASSES * M], U32, align_bytes=64)
         w_scales = const.tile([P, PASSES * M], U8, align_bytes=64)
         w_words = w_raw[:].bitcast(F32)
-        for t in range(W_TILES):
+
+        def regroup_w(t):
             w_bank = psum_y.tile([P, BANK], F32, name="y")
             transpose_rows(w_words[:, t * WORDS : (t + 1) * WORDS], w_bank)
             target = w_grouped_words[:, :, t * P : (t + 1) * P, :]
@@ -118,15 +124,15 @@ def tile_linearattention_pa_kernel(tc, feature, aspect_v, W, b, out_0, out_1):
                 nc.scalar.copy(out=target, in_=pairs_side_by_side(w_bank))
             else:
                 nc.vector.tensor_copy(out=target, in_=pairs_side_by_side(w_bank))
-            if (t + 1) % (BANK // P) == 0:
-                h = t // (BANK // P)
-                for c in range(PASSES):
-                    lo = c * M + h * BANK
-                    nc.vector.quantize_mx(
-                        out=w_codes[:, lo : lo + BANK].bitcast(FP8X4),
-                        scales=w_scales[:, lo : lo + BANK],
-                        in_=w_grouped[:, 4 * lo : 4 * (lo + BANK)],
-                    )
+
+        def quantise_w(h):
+            for c in range(PASSES):
+                lo = c * M + h * BANK
+                nc.vector.quantize_mx(
+                    out=w_codes[:, lo : lo + BANK].bitcast(FP8X4),
+                    scales=w_scales[:, lo : lo + BANK],
+                    in_=w_grouped[:, 4 * lo : 4 * (lo + BANK)],
+                )
 
         grouped = {}
         codes = {}
@@ -153,9 +159,10 @@ def tile_linearattention_pa_kernel(tc, feature, aspect_v, W, b, out_0, out_1):
                 out=codes[i][:].bitcast(FP8X4), scales=scales[i][:], in_=grouped[i][:]
             )
 
-        def multiply_and_add_bias(i):
-            z[i] = z_pool.tile([P, M], F32, name="z")
-            for h in range(HALVES):
+        def multiply_and_add_bias(i, halves=range(HALVES)):
+            if 0 in halves:
+                z[i] = z_pool.tile([P, M], F32, name="z")
+            for h in halves:
                 y = psum_y.tile([P, BANK], F32, name="y")
                 for c in range(PASSES):
                     rows = slice(c * P, (c + 1) * P)
@@ -173,46 +180,89 @@ def tile_linearattention_pa_kernel(tc, feature, aspect_v, W, b, out_0, out_1):
                 nc.vector.tensor_tensor(out=z[i][:, half], in0=y[:], in1=bias[:, half], op=ALU.add)
 
         def sum_of_squares(i):
-            sumsq[i] = norm_pool.tile([P, 1], F32, name="sumsq")
+            factor = 1.0 if i % TILES_PER_GROUP == ASPECT else float(TOKENS)
+            parts = HALVES if i == ROW_TILES - 1 else 1
+            width = M // parts
+            sumsq[i] = norm_pool.tile([P, HALVES], F32, name="sumsq")
             squares = scratch_pool.tile([P, M], F32, name="squares")
-            nc.scalar.activation(out=squares[:], in_=z[i][:], func=ACT.Square, accum_out=sumsq[i][:])
+            for n in range(parts):
+                cols = slice(n * width, (n + 1) * width)
+                nc.scalar.activation(
+                    out=squares[:, cols], in_=z[i][:, cols], func=ACT.Square, scale=factor,
+                    accum_out=sumsq[i][:, n : n + 1],
+                )
 
         def reciprocal_norm(i):
-            t = i % TILES_PER_GROUP
+            floor = 1e-24 if i % TILES_PER_GROUP == ASPECT else 1e-24 * TOKENS * TOKENS
             clamped = norm_pool.tile([P, 1], F32, name="clamped")
-            nc.gpsimd.tensor_scalar(
-                out=clamped[:], in0=sumsq[i][:], scalar1=1e-24,
-                scalar2=(1.0 if t == 0 else float(TOKENS * TOKENS)), op0=ALU.max, op1=ALU.mult,
-            )
+            if i == ROW_TILES - 1:
+                nc.gpsimd.tensor_scalar(
+                    out=clamped[:], in0=sumsq[i][:, 0:1], scalar1=sumsq[i][:, 1:2], scalar2=floor,
+                    op0=ALU.add, op1=ALU.max,
+                )
+            else:
+                nc.gpsimd.tensor_scalar_max(clamped[:], sumsq[i][:, 0:1], floor)
             rnorm[i] = norm_pool.tile([P, 1], F32, name="rnorm")
             nc.gpsimd.tensor_tensor(out=rnorm[i][:], in0=clamped[:], in1=minus_half[:], op=ALU.pow)
 
         def scale(i):
             g, t = divmod(i, TILES_PER_GROUP)
+            last = g == GROUPS - 1
             if t == 0:
-                q = out_pool.tile([P, M], F32, name="q")
-                nc.scalar.activation(out=q[:], in_=z[i][:], func=ACT.Copy, scale=rnorm[i][:])
-                nc.sync.dma_start(out=out_0[g * P : (g + 1) * P, :], in_=q[:])
-            if t == 1:
                 fm[g] = out_pool.tile([P, M], F32, name="fm")
-                nc.scalar.activation(out=fm[g][:], in_=z[i][:], func=ACT.Copy, scale=rnorm[i][:])
+                if last:
+                    nc.vector.tensor_scalar_mul(fm[g][:], z[i][:], rnorm[i][:])
+                else:
+                    nc.scalar.activation(out=fm[g][:], in_=z[i][:], func=ACT.Copy, scale=rnorm[i][:])
+            if t == ASPECT:
+                segments = slice(g * P, (g + 1) * P)
+                if last:
+                    for h in range(HALVES):
+                        half = slice(h * BANK, (h + 1) * BANK)
+                        q = out_pool.tile([P, BANK], F32, name=f"q_half_{h}")
+                        if h == 0:
+                            nc.vector.tensor_scalar_mul(q[:], z[i][:, half], rnorm[i][:])
+                        else:
+                            nc.scalar.activation(out=q[:], in_=z[i][:, half], func=ACT.Copy, scale=rnorm[i][:])
+                        nc.sync.dma_start(out=out_0[segments, half], in_=q[:])
+                else:
+                    q = out_pool.tile([P, M], F32, name="q")
+                    nc.scalar.activation(out=q[:], in_=z[i][:], func=ACT.Copy, scale=rnorm[i][:])
+                    nc.sync.dma_start(out=out_0[segments, :], in_=q[:])
 
         def add_to_mean(i):
             g, t = divmod(i, TILES_PER_GROUP)
-            if t >= 2:
+            if 1 <= t < TOKENS:
                 nc.vector.scalar_tensor_tensor(
                     out=fm[g][:], in0=z[i][:], scalar=rnorm[i][:], in1=fm[g][:],
                     op0=ALU.mult, op1=ALU.add,
                 )
-            if t == TILES_PER_GROUP - 1:
+            if t == TOKENS - 1:
                 nc.sync.dma_start(out=out_1[g * P : (g + 1) * P, :], in_=fm[g][:])
 
-        for step in range(-AHEAD_TRANSPOSE, ROW_TILES + BEHIND_MEAN):
-            if 0 <= step < ROW_TILES:
-                multiply_and_add_bias(step)
+        for t in range(W_TILES // 2):
+            regroup_w(t)
+        transpose_and_regroup(0)
+        quantise_w(0)
+        spread_bias()
+        quantise(0)
+        transpose_and_regroup(1)
+        multiply_and_add_bias(0, [0])
+        regroup_w(4)
+        regroup_w(5)
+        quantise(1)
+        multiply_and_add_bias(1, [0])
+        regroup_w(6)
+        regroup_w(7)
+        transpose_and_regroup(2)
+        quantise_w(1)
+        transpose_and_regroup(3)
+        for step in range(ROW_TILES + BEHIND_MEAN):
+            if step < ROW_TILES:
+                multiply_and_add_bias(step, [1] if step < EARLY else range(HALVES))
             if step + AHEAD_TRANSPOSE < ROW_TILES:
                 transpose_and_regroup(step + AHEAD_TRANSPOSE)
-            if 0 <= step + AHEAD_QUANTISE < ROW_TILES:
+            if step + AHEAD_QUANTISE < ROW_TILES:
                 quantise(step + AHEAD_QUANTISE)
             if 0 <= step - BEHIND_NORM < ROW_TILES:
                 sum_of_squares(step - BEHIND_NORM)

@@ -240,6 +240,7 @@ def tile_linearattention_pa_kernel(tc, feature, aspect_v, W, b, out_0, out_1):
             if t == TOKENS - 1:
                 nc.sync.dma_start(out=out_1[g * P : (g + 1) * P, :], in_=fm[g][:])
 
+        stack.enter_context(tc.manual_schedule(engines={mybir.EngineType.PE}))
         for t in range(W_TILES // 2):
             regroup_w(t)
         transpose_and_regroup(0)
@@ -258,10 +259,13 @@ def tile_linearattention_pa_kernel(tc, feature, aspect_v, W, b, out_0, out_1):
         quantise_w(1)
         transpose_and_regroup(3)
         for step in range(ROW_TILES + BEHIND_MEAN):
-            if step < ROW_TILES:
-                multiply_and_add_bias(step, [1] if step < EARLY else range(HALVES))
-            if step + AHEAD_TRANSPOSE < ROW_TILES:
-                transpose_and_regroup(step + AHEAD_TRANSPOSE)
+            if step % 2 == 0:
+                for i in (step, step + 1):
+                    if i < ROW_TILES:
+                        multiply_and_add_bias(i, [1] if i < EARLY else range(HALVES))
+                for i in (step + AHEAD_TRANSPOSE, step + AHEAD_TRANSPOSE + 1):
+                    if i < ROW_TILES:
+                        transpose_and_regroup(i)
             if step + AHEAD_QUANTISE < ROW_TILES:
                 quantise(step + AHEAD_QUANTISE)
             if 0 <= step - BEHIND_NORM < ROW_TILES:

@@ -27,12 +27,9 @@ ASPECT = TOKENS
 ROW_TILES = GROUPS * TILES_PER_GROUP
 W_TILES = M // P
 
-EARLY = 2
-AHEAD_TRANSPOSE = 4
-AHEAD_QUANTISE = 2
-BEHIND_NORM = 1
-BEHIND_SCALE = 3
-BEHIND_MEAN = 4
+PAIR = 2
+PAIRS = ROW_TILES // PAIR
+BEHIND_CLOSE = 3
 
 FLOPS = 2 * (SEGMENTS * TOKENS + SEGMENTS) * K * M
 
@@ -42,9 +39,9 @@ def tile_linearattention_pa_kernel(tc, feature, aspect_v, W, b, out_0, out_1):
     with ExitStack() as stack:
         const = stack.enter_context(tc.tile_pool(name="const", bufs=1))
         raw_pool = stack.enter_context(tc.tile_pool(name="raw", bufs=GROUPS))
-        grouped_pool = stack.enter_context(tc.tile_pool(name="grouped", bufs=4))
+        grouped_pool = stack.enter_context(tc.tile_pool(name="grouped", bufs=3))
         mx_pool = stack.enter_context(tc.tile_pool(name="mx", bufs=4))
-        z_pool = stack.enter_context(tc.tile_pool(name="z", bufs=9))
+        z_pool = stack.enter_context(tc.tile_pool(name="z", bufs=12))
         scratch_pool = stack.enter_context(tc.tile_pool(name="scratch", bufs=2))
         norm_pool = stack.enter_context(tc.tile_pool(name="norm", bufs=9))
         out_pool = stack.enter_context(tc.tile_pool(name="out", bufs=2))
@@ -80,10 +77,10 @@ def tile_linearattention_pa_kernel(tc, feature, aspect_v, W, b, out_0, out_1):
         load_w(2)
         load_rows(0)
         nc.sync.dma_start(out=bias_row[0:1, :], in_=b.rearrange("(o m) -> o m", o=1))
-        load_rows(1)
         load_w(4)
+        load_rows(1)
         load_w(6)
-        for i in range(EARLY, ROW_TILES):
+        for i in range(PAIR, ROW_TILES):
             load_rows(i)
 
         def transpose_rows(words, bank):
@@ -116,14 +113,10 @@ def tile_linearattention_pa_kernel(tc, feature, aspect_v, W, b, out_0, out_1):
         w_scales = const.tile([P, PASSES * M], U8, align_bytes=64)
         w_words = w_raw[:].bitcast(F32)
 
-        def regroup_w(t):
+        def regroup_w(t, copy):
             w_bank = psum_y.tile([P, BANK], F32, name="y")
             transpose_rows(w_words[:, t * WORDS : (t + 1) * WORDS], w_bank)
-            target = w_grouped_words[:, :, t * P : (t + 1) * P, :]
-            if t % 2 == 0:
-                nc.scalar.copy(out=target, in_=pairs_side_by_side(w_bank))
-            else:
-                nc.vector.tensor_copy(out=target, in_=pairs_side_by_side(w_bank))
+            copy(out=w_grouped_words[:, :, t * P : (t + 1) * P, :], in_=pairs_side_by_side(w_bank))
 
         def quantise_w(h):
             for c in range(PASSES):
@@ -134,6 +127,7 @@ def tile_linearattention_pa_kernel(tc, feature, aspect_v, W, b, out_0, out_1):
                     in_=w_grouped[:, 4 * lo : 4 * (lo + BANK)],
                 )
 
+        x_bank = {}
         grouped = {}
         codes = {}
         scales = {}
@@ -142,42 +136,52 @@ def tile_linearattention_pa_kernel(tc, feature, aspect_v, W, b, out_0, out_1):
         rnorm = {}
         fm = {}
 
-        def transpose_and_regroup(i):
+        def transpose(i):
             g, t = divmod(i, TILES_PER_GROUP)
-            x_bank = psum_t.tile([P, BANK], F32, name="xt")
-            transpose_rows(raw[g][:].bitcast(F32)[:, t * WORDS : (t + 1) * WORDS], x_bank)
-            grouped[i] = grouped_pool.tile([P, 2 * WORDS], BF16, name="grouped", align_bytes=64)
+            x_bank[i] = psum_t.tile([P, BANK], F32, name="xt")
+            transpose_rows(raw[g][:].bitcast(F32)[:, t * WORDS : (t + 1) * WORDS], x_bank[i])
+
+        def regroup(i):
+            k, n = divmod(i, PAIR)
+            if n == 0:
+                grouped[k] = grouped_pool.tile([P, PAIR * K], BF16, name="grouped", align_bytes=64)
             nc.scalar.copy(
-                out=grouped[i][:].bitcast(F32).rearrange("p (c r u) -> p c r u", c=PASSES, u=2),
-                in_=pairs_side_by_side(x_bank),
+                out=grouped[k][:, n * K : (n + 1) * K]
+                .bitcast(F32)
+                .rearrange("p (c r u) -> p c r u", c=PASSES, u=2),
+                in_=pairs_side_by_side(x_bank[i]),
             )
 
-        def quantise(i):
-            codes[i] = mx_pool.tile([P, PASSES * P], U32, name="codes", align_bytes=64)
-            scales[i] = mx_pool.tile([P, PASSES * P], U8, name="scales", align_bytes=64)
+        def quantise(k, tiles=(0, PAIR)):
+            if tiles[0] == 0:
+                codes[k] = mx_pool.tile([P, PAIR * PASSES * P], U32, name="codes", align_bytes=64)
+                scales[k] = mx_pool.tile([P, PAIR * PASSES * P], U8, name="scales", align_bytes=64)
+            cols = slice(tiles[0] * PASSES * P, tiles[1] * PASSES * P)
             nc.vector.quantize_mx(
-                out=codes[i][:].bitcast(FP8X4), scales=scales[i][:], in_=grouped[i][:]
+                out=codes[k][:, cols].bitcast(FP8X4),
+                scales=scales[k][:, cols],
+                in_=grouped[k][:, tiles[0] * K : tiles[1] * K],
             )
 
-        def multiply_and_add_bias(i, halves=range(HALVES)):
-            if 0 in halves:
+        def multiply_and_add_bias(i, h):
+            k, n = divmod(i, PAIR)
+            if h == 0:
                 z[i] = z_pool.tile([P, M], F32, name="z")
-            for h in halves:
-                y = psum_y.tile([P, BANK], F32, name="y")
-                for c in range(PASSES):
-                    rows = slice(c * P, (c + 1) * P)
-                    cols = slice(c * M + h * BANK, c * M + (h + 1) * BANK)
-                    nc.tensor.matmul_mx(
-                        out=y[:],
-                        lhsT=codes[i][:, rows].bitcast(FP8X4),
-                        lhsT_scale=scales[i][:, rows],
-                        rhs=w_codes[:, cols].bitcast(FP8X4),
-                        rhs_scale=w_scales[:, cols],
-                        start=(c == 0),
-                        stop=(c == PASSES - 1),
-                    )
-                half = slice(h * BANK, (h + 1) * BANK)
-                nc.vector.tensor_tensor(out=z[i][:, half], in0=y[:], in1=bias[:, half], op=ALU.add)
+            y = psum_y.tile([P, BANK], F32, name="y")
+            for c in range(PASSES):
+                rows = slice((n * PASSES + c) * P, (n * PASSES + c + 1) * P)
+                cols = slice(c * M + h * BANK, c * M + (h + 1) * BANK)
+                nc.tensor.matmul_mx(
+                    out=y[:],
+                    lhsT=codes[k][:, rows].bitcast(FP8X4),
+                    lhsT_scale=scales[k][:, rows],
+                    rhs=w_codes[:, cols].bitcast(FP8X4),
+                    rhs_scale=w_scales[:, cols],
+                    start=(c == 0),
+                    stop=(c == PASSES - 1),
+                )
+            half = slice(h * BANK, (h + 1) * BANK)
+            nc.vector.tensor_tensor(out=z[i][:, half], in0=y[:], in1=bias[:, half], op=ALU.add)
 
         def sum_of_squares(i):
             factor = 1.0 if i % TILES_PER_GROUP == ASPECT else float(TOKENS)
@@ -240,38 +244,52 @@ def tile_linearattention_pa_kernel(tc, feature, aspect_v, W, b, out_0, out_1):
             if t == TOKENS - 1:
                 nc.sync.dma_start(out=out_1[g * P : (g + 1) * P, :], in_=fm[g][:])
 
-        stack.enter_context(tc.manual_schedule(engines={mybir.EngineType.PE}))
+        engines = {mybir.EngineType.PE, mybir.EngineType.DVE, mybir.EngineType.Activation}
+        stack.enter_context(tc.manual_schedule(engines=engines))
+
         for t in range(W_TILES // 2):
-            regroup_w(t)
-        transpose_and_regroup(0)
+            regroup_w(t, nc.scalar.copy if t % 2 == 0 else nc.vector.tensor_copy)
         quantise_w(0)
+        transpose(0)
+        regroup(0)
+        quantise(0, (0, 1))
         spread_bias()
-        quantise(0)
-        transpose_and_regroup(1)
-        multiply_and_add_bias(0, [0])
-        regroup_w(4)
-        regroup_w(5)
-        quantise(1)
-        multiply_and_add_bias(1, [0])
-        regroup_w(6)
-        regroup_w(7)
-        transpose_and_regroup(2)
+        regroup_w(4, nc.scalar.copy)
+        regroup_w(5, nc.scalar.copy)
+        transpose(1)
+        regroup(1)
+        quantise(0, (1, 2))
+        regroup_w(6, nc.scalar.copy)
+        regroup_w(7, nc.scalar.copy)
+        multiply_and_add_bias(0, 0)
+        multiply_and_add_bias(1, 0)
+        transpose(2)
+        transpose(3)
+        regroup(2)
+        regroup(3)
         quantise_w(1)
-        transpose_and_regroup(3)
-        for step in range(ROW_TILES + BEHIND_MEAN):
-            if step % 2 == 0:
-                for i in (step, step + 1):
-                    if i < ROW_TILES:
-                        multiply_and_add_bias(i, [1] if i < EARLY else range(HALVES))
-                for i in (step + AHEAD_TRANSPOSE, step + AHEAD_TRANSPOSE + 1):
-                    if i < ROW_TILES:
-                        transpose_and_regroup(i)
-            if step + AHEAD_QUANTISE < ROW_TILES:
-                quantise(step + AHEAD_QUANTISE)
-            if 0 <= step - BEHIND_NORM < ROW_TILES:
-                sum_of_squares(step - BEHIND_NORM)
-                reciprocal_norm(step - BEHIND_NORM)
-            if 0 <= step - BEHIND_SCALE < ROW_TILES:
-                scale(step - BEHIND_SCALE)
-            if 0 <= step - BEHIND_MEAN < ROW_TILES:
-                add_to_mean(step - BEHIND_MEAN)
+        quantise(1)
+        transpose(4)
+        transpose(5)
+
+        for k in range(PAIRS + BEHIND_CLOSE):
+            if k + 2 < PAIRS:
+                for n in range(PAIR):
+                    regroup(PAIR * (k + 2) + n)
+            for n in range(PAIR):
+                i = PAIR * k + n
+                if k < PAIRS:
+                    for h in range(HALVES):
+                        if k > 0 or h > 0:
+                            multiply_and_add_bias(i, h)
+                if n == 1 and k + 2 < PAIRS:
+                    quantise(k + 2)
+                if 0 <= i - PAIR < ROW_TILES:
+                    sum_of_squares(i - PAIR)
+                    reciprocal_norm(i - PAIR)
+                if k >= BEHIND_CLOSE:
+                    scale(i - PAIR * BEHIND_CLOSE)
+                    add_to_mean(i - PAIR * BEHIND_CLOSE)
+            if k + 3 < PAIRS:
+                for n in range(PAIR):
+                    transpose(PAIR * (k + 3) + n)

@@ -23,13 +23,27 @@ BANK = 512
 HALVES = M // BANK
 GROUPS = SEGMENTS // P
 TILES_PER_GROUP = TOKENS + 1
-ASPECT = TOKENS
 ROW_TILES = GROUPS * TILES_PER_GROUP
+ASPECT = TOKENS
+ASPECT_LAG = 2
+
+
+def row_tile_order():
+    order = []
+    for g in range(GROUPS + ASPECT_LAG):
+        if g < GROUPS:
+            order += [(g, t) for t in range(TOKENS)]
+        if g >= ASPECT_LAG:
+            order += [(g - ASPECT_LAG, ASPECT)]
+    return order
+
+
+ORDER = row_tile_order()
 W_TILES = M // P
 
 PAIR = 2
 PAIRS = ROW_TILES // PAIR
-BEHIND_CLOSE = 3
+BEHIND_CLOSE = 2
 
 FLOPS = 2 * (SEGMENTS * TOKENS + SEGMENTS) * K * M
 
@@ -38,11 +52,11 @@ def tile_linearattention_pa_kernel(tc, feature, aspect_v, W, b, out_0, out_1):
     nc = tc.nc
     with ExitStack() as stack:
         const = stack.enter_context(tc.tile_pool(name="const", bufs=1))
-        raw_pool = stack.enter_context(tc.tile_pool(name="raw", bufs=GROUPS))
+        raw_pool = stack.enter_context(tc.tile_pool(name="raw", bufs=28))
         grouped_pool = stack.enter_context(tc.tile_pool(name="grouped", bufs=3))
         mx_pool = stack.enter_context(tc.tile_pool(name="mx", bufs=4))
         z_pool = stack.enter_context(tc.tile_pool(name="z", bufs=12))
-        scratch_pool = stack.enter_context(tc.tile_pool(name="scratch", bufs=2))
+        scratch_pool = stack.enter_context(tc.tile_pool(name="scratch", bufs=8))
         norm_pool = stack.enter_context(tc.tile_pool(name="norm", bufs=9))
         out_pool = stack.enter_context(tc.tile_pool(name="out", bufs=2))
         psum_t = stack.enter_context(tc.psum_pool(name="psum_t", bufs=2))
@@ -61,25 +75,25 @@ def tile_linearattention_pa_kernel(tc, feature, aspect_v, W, b, out_0, out_1):
         w_raw_tiles = w_raw[:].rearrange("p (t k) -> p t k", k=K)
         w_rows = W.rearrange("(t p) k -> p t k", p=P)
         raw = {}
-        for g in range(GROUPS):
-            raw[g] = raw_pool.tile([P, TILES_PER_GROUP * K], BF16, name="raw")
 
-        def load_w(t):
-            nc.sync.dma_start(out=w_raw_tiles[:, t : t + 2, :], in_=w_rows[:, t : t + 2, :])
+        def load_w(t, tiles):
+            nc.sync.dma_start(out=w_raw_tiles[:, t : t + tiles, :], in_=w_rows[:, t : t + tiles, :])
 
         def load_rows(i):
-            g, t = divmod(i, TILES_PER_GROUP)
+            g, t = ORDER[i]
             segments = slice(g * P, (g + 1) * P)
             rows = aspect_v[segments, :] if t == ASPECT else feature[segments, t, :]
-            nc.sync.dma_start(out=raw[g][:, t * K : (t + 1) * K], in_=rows)
+            raw[i] = raw_pool.tile([P, K], BF16, name="raw")
+            nc.sync.dma_start(out=raw[i][:], in_=rows)
 
-        load_w(0)
-        load_w(2)
+        load_w(0, 1)
+        load_w(1, 1)
+        load_w(2, 2)
         load_rows(0)
         nc.sync.dma_start(out=bias_row[0:1, :], in_=b.rearrange("(o m) -> o m", o=1))
-        load_w(4)
+        load_w(4, 2)
         load_rows(1)
-        load_w(6)
+        load_w(6, 2)
         for i in range(PAIR, ROW_TILES):
             load_rows(i)
 
@@ -131,19 +145,19 @@ def tile_linearattention_pa_kernel(tc, feature, aspect_v, W, b, out_0, out_1):
         grouped = {}
         codes = {}
         scales = {}
+        y_bank = {}
         z = {}
         sumsq = {}
         rnorm = {}
         fm = {}
 
         def transpose(i):
-            g, t = divmod(i, TILES_PER_GROUP)
             x_bank[i] = psum_t.tile([P, BANK], F32, name="xt")
-            transpose_rows(raw[g][:].bitcast(F32)[:, t * WORDS : (t + 1) * WORDS], x_bank[i])
+            transpose_rows(raw[i][:].bitcast(F32), x_bank[i])
 
         def regroup(i):
             k, n = divmod(i, PAIR)
-            if n == 0:
+            if k not in grouped:
                 grouped[k] = grouped_pool.tile([P, PAIR * K], BF16, name="grouped", align_bytes=64)
             nc.scalar.copy(
                 out=grouped[k][:, n * K : (n + 1) * K]
@@ -163,10 +177,8 @@ def tile_linearattention_pa_kernel(tc, feature, aspect_v, W, b, out_0, out_1):
                 in_=grouped[k][:, tiles[0] * K : tiles[1] * K],
             )
 
-        def multiply_and_add_bias(i, h):
+        def multiply(i, h):
             k, n = divmod(i, PAIR)
-            if h == 0:
-                z[i] = z_pool.tile([P, M], F32, name="z")
             y = psum_y.tile([P, BANK], F32, name="y")
             for c in range(PASSES):
                 rows = slice((n * PASSES + c) * P, (n * PASSES + c + 1) * P)
@@ -180,11 +192,16 @@ def tile_linearattention_pa_kernel(tc, feature, aspect_v, W, b, out_0, out_1):
                     start=(c == 0),
                     stop=(c == PASSES - 1),
                 )
+            y_bank[i, h] = y
+
+        def add_bias(i, h):
+            if i not in z:
+                z[i] = z_pool.tile([P, M], F32, name="z")
             half = slice(h * BANK, (h + 1) * BANK)
-            nc.vector.tensor_tensor(out=z[i][:, half], in0=y[:], in1=bias[:, half], op=ALU.add)
+            nc.vector.tensor_tensor(out=z[i][:, half], in0=y_bank[i, h][:], in1=bias[:, half], op=ALU.add)
 
         def sum_of_squares(i):
-            factor = 1.0 if i % TILES_PER_GROUP == ASPECT else float(TOKENS)
+            factor = 1.0 if ORDER[i][1] == ASPECT else float(TOKENS)
             parts = HALVES if i == ROW_TILES - 1 else 1
             width = M // parts
             sumsq[i] = norm_pool.tile([P, HALVES], F32, name="sumsq")
@@ -197,7 +214,7 @@ def tile_linearattention_pa_kernel(tc, feature, aspect_v, W, b, out_0, out_1):
                 )
 
         def reciprocal_norm(i):
-            floor = 1e-24 if i % TILES_PER_GROUP == ASPECT else 1e-24 * TOKENS * TOKENS
+            floor = 1e-24 if ORDER[i][1] == ASPECT else 1e-24 * TOKENS * TOKENS
             clamped = norm_pool.tile([P, 1], F32, name="clamped")
             if i == ROW_TILES - 1:
                 nc.gpsimd.tensor_scalar(
@@ -210,17 +227,20 @@ def tile_linearattention_pa_kernel(tc, feature, aspect_v, W, b, out_0, out_1):
             nc.gpsimd.tensor_tensor(out=rnorm[i][:], in0=clamped[:], in1=minus_half[:], op=ALU.pow)
 
         def scale(i):
-            g, t = divmod(i, TILES_PER_GROUP)
-            last = g == GROUPS - 1
+            g, t = ORDER[i]
             if t == 0:
                 fm[g] = out_pool.tile([P, M], F32, name="fm")
-                if last:
-                    nc.vector.tensor_scalar_mul(fm[g][:], z[i][:], rnorm[i][:])
-                else:
-                    nc.scalar.activation(out=fm[g][:], in_=z[i][:], func=ACT.Copy, scale=rnorm[i][:])
+                nc.scalar.activation(out=fm[g][:], in_=z[i][:], func=ACT.Copy, scale=rnorm[i][:])
             if t == ASPECT:
                 segments = slice(g * P, (g + 1) * P)
-                if last:
+                if i in (ROW_TILES - 3, ROW_TILES - 2):
+                    q = out_pool.tile([P, M], F32, name="q")
+                    if i == ROW_TILES - 3:
+                        nc.vector.tensor_scalar_mul(q[:], z[i][:], rnorm[i][:])
+                    else:
+                        nc.scalar.activation(out=q[:], in_=z[i][:], func=ACT.Copy, scale=rnorm[i][:])
+                    nc.sync.dma_start(out=out_0[segments, :], in_=q[:])
+                elif i == ROW_TILES - 1:
                     for h in range(HALVES):
                         half = slice(h * BANK, (h + 1) * BANK)
                         q = out_pool.tile([P, BANK], F32, name=f"q_half_{h}")
@@ -230,12 +250,14 @@ def tile_linearattention_pa_kernel(tc, feature, aspect_v, W, b, out_0, out_1):
                             nc.scalar.activation(out=q[:], in_=z[i][:, half], func=ACT.Copy, scale=rnorm[i][:])
                         nc.sync.dma_start(out=out_0[segments, half], in_=q[:])
                 else:
-                    q = out_pool.tile([P, M], F32, name="q")
-                    nc.scalar.activation(out=q[:], in_=z[i][:], func=ACT.Copy, scale=rnorm[i][:])
+                    q = z[i - 1]
+                    nc.gpsimd.tensor_scalar(
+                        out=q[:], in0=z[i][:], scalar1=rnorm[i][:], scalar2=0.0, op0=ALU.mult, op1=ALU.add
+                    )
                     nc.sync.dma_start(out=out_0[segments, :], in_=q[:])
 
         def add_to_mean(i):
-            g, t = divmod(i, TILES_PER_GROUP)
+            g, t = ORDER[i]
             if 1 <= t < TOKENS:
                 nc.vector.scalar_tensor_tensor(
                     out=fm[g][:], in0=z[i][:], scalar=rnorm[i][:], in1=fm[g][:],
@@ -255,38 +277,43 @@ def tile_linearattention_pa_kernel(tc, feature, aspect_v, W, b, out_0, out_1):
         quantise(0, (0, 1))
         spread_bias()
         regroup_w(4, nc.scalar.copy)
-        regroup_w(5, nc.scalar.copy)
+        regroup_w(5, nc.vector.tensor_copy)
         transpose(1)
         regroup(1)
         quantise(0, (1, 2))
         regroup_w(6, nc.scalar.copy)
-        regroup_w(7, nc.scalar.copy)
-        multiply_and_add_bias(0, 0)
-        multiply_and_add_bias(1, 0)
+        regroup_w(7, nc.vector.tensor_copy)
+        multiply(0, 0)
+        add_bias(0, 0)
+        quantise_w(1)
+        multiply(1, 0)
+        add_bias(1, 0)
         transpose(2)
         transpose(3)
         regroup(2)
         regroup(3)
-        quantise_w(1)
         quantise(1)
         transpose(4)
         transpose(5)
 
         for k in range(PAIRS + BEHIND_CLOSE):
             if k + 2 < PAIRS:
-                for n in range(PAIR):
+                for n in (1, 0):
                     regroup(PAIR * (k + 2) + n)
+            if 0 < k <= PAIRS:
+                for n in range(PAIR):
+                    sum_of_squares(PAIR * (k - 1) + n)
+                    reciprocal_norm(PAIR * (k - 1) + n)
             for n in range(PAIR):
                 i = PAIR * k + n
                 if k < PAIRS:
-                    for h in range(HALVES):
-                        if k > 0 or h > 0:
-                            multiply_and_add_bias(i, h)
+                    halves = [h for h in range(HALVES) if k > 0 or h > 0]
+                    for h in halves:
+                        multiply(i, h)
+                    for h in reversed(halves):
+                        add_bias(i, h)
                 if n == 1 and k + 2 < PAIRS:
                     quantise(k + 2)
-                if 0 <= i - PAIR < ROW_TILES:
-                    sum_of_squares(i - PAIR)
-                    reciprocal_norm(i - PAIR)
                 if k >= BEHIND_CLOSE:
                     scale(i - PAIR * BEHIND_CLOSE)
                     add_to_mean(i - PAIR * BEHIND_CLOSE)

@@ -25,7 +25,7 @@ GROUPS = SEGMENTS // P
 TILES_PER_GROUP = TOKENS + 1
 ROW_TILES = GROUPS * TILES_PER_GROUP
 ASPECT = TOKENS
-ASPECT_LAG = 2
+ASPECT_LAG = 1
 
 
 def row_tile_order():
@@ -43,7 +43,7 @@ W_TILES = M // P
 
 PAIR = 2
 PAIRS = ROW_TILES // PAIR
-BEHIND_CLOSE = 2
+BEHIND_CLOSE = 3
 
 FLOPS = 2 * (SEGMENTS * TOKENS + SEGMENTS) * K * M
 
@@ -60,12 +60,13 @@ def tile_linearattention_pa_kernel(tc, feature, aspect_v, W, b, out_0, out_1):
         norm_pool = stack.enter_context(tc.tile_pool(name="norm", bufs=9))
         out_pool = stack.enter_context(tc.tile_pool(name="out", bufs=2))
         psum_t = stack.enter_context(tc.psum_pool(name="psum_t", bufs=2))
-        psum_y = stack.enter_context(tc.psum_pool(name="psum_y", bufs=6))
+        psum_y = stack.enter_context(tc.psum_pool(name="psum_y", bufs=5))
+        psum_idle = stack.enter_context(tc.psum_pool(name="psum_idle", bufs=1))
 
+        ones = const.tile([P, BANK], BF16)
+        nc.vector.memset(ones[:], 1.0)
         bias_row = const.tile([P, M], BF16)
         nc.vector.memset(bias_row[:], 0.0)
-        ones = const.tile([P, P], BF16)
-        nc.vector.memset(ones[:], 1.0)
         minus_half = const.tile([P, 1], F32)
         nc.vector.memset(minus_half[:], -0.5)
         identity = const.tile([P, P], F32)
@@ -97,6 +98,12 @@ def tile_linearattention_pa_kernel(tc, feature, aspect_v, W, b, out_0, out_1):
         for i in range(PAIR, ROW_TILES):
             load_rows(i)
 
+        idle_bank = psum_idle.tile([P, BANK], F32)
+
+        def keep_clock(passes):
+            for n in range(passes):
+                nc.tensor.matmul(out=idle_bank[:], lhsT=ones[:, 0:P], rhs=ones[:], start=True, stop=True)
+
         def transpose_rows(words, bank):
             for c in range(PASSES):
                 for u in range(2):
@@ -116,7 +123,7 @@ def tile_linearattention_pa_kernel(tc, feature, aspect_v, W, b, out_0, out_1):
             b_bank = psum_y.tile([P, M], BF16, name="y")
             for h in range(HALVES):
                 half = slice(h * BANK, (h + 1) * BANK)
-                nc.tensor.matmul(out=b_bank[:, half], lhsT=ones[:], rhs=bias_row[:, half], start=True, stop=True)
+                nc.tensor.matmul(out=b_bank[:, half], lhsT=ones[:, 0:P], rhs=bias_row[:, half], start=True, stop=True)
             nc.scalar.copy(out=bias[:], in_=b_bank[:])
 
         w_grouped = const.tile([P, PASSES * M * 4], BF16, align_bytes=64)
@@ -233,14 +240,7 @@ def tile_linearattention_pa_kernel(tc, feature, aspect_v, W, b, out_0, out_1):
                 nc.scalar.activation(out=fm[g][:], in_=z[i][:], func=ACT.Copy, scale=rnorm[i][:])
             if t == ASPECT:
                 segments = slice(g * P, (g + 1) * P)
-                if i in (ROW_TILES - 3, ROW_TILES - 2):
-                    q = out_pool.tile([P, M], F32, name="q")
-                    if i == ROW_TILES - 3:
-                        nc.vector.tensor_scalar_mul(q[:], z[i][:], rnorm[i][:])
-                    else:
-                        nc.scalar.activation(out=q[:], in_=z[i][:], func=ACT.Copy, scale=rnorm[i][:])
-                    nc.sync.dma_start(out=out_0[segments, :], in_=q[:])
-                elif i == ROW_TILES - 1:
+                if i == ROW_TILES - 1:
                     for h in range(HALVES):
                         half = slice(h * BANK, (h + 1) * BANK)
                         q = out_pool.tile([P, BANK], F32, name=f"q_half_{h}")
@@ -250,10 +250,8 @@ def tile_linearattention_pa_kernel(tc, feature, aspect_v, W, b, out_0, out_1):
                             nc.scalar.activation(out=q[:], in_=z[i][:, half], func=ACT.Copy, scale=rnorm[i][:])
                         nc.sync.dma_start(out=out_0[segments, half], in_=q[:])
                 else:
-                    q = z[i - 1]
-                    nc.gpsimd.tensor_scalar(
-                        out=q[:], in0=z[i][:], scalar1=rnorm[i][:], scalar2=0.0, op0=ALU.mult, op1=ALU.add
-                    )
+                    q = out_pool.tile([P, M], F32, name="q")
+                    nc.scalar.activation(out=q[:], in_=z[i][:], func=ACT.Copy, scale=rnorm[i][:])
                     nc.sync.dma_start(out=out_0[segments, :], in_=q[:])
 
         def add_to_mean(i):
@@ -269,8 +267,11 @@ def tile_linearattention_pa_kernel(tc, feature, aspect_v, W, b, out_0, out_1):
         engines = {mybir.EngineType.PE, mybir.EngineType.DVE, mybir.EngineType.Activation}
         stack.enter_context(tc.manual_schedule(engines=engines))
 
+        keep_clock(5)
         for t in range(W_TILES // 2):
             regroup_w(t, nc.scalar.copy if t % 2 == 0 else nc.vector.tensor_copy)
+            if t % 2 == 1:
+                keep_clock(1)
         quantise_w(0)
         transpose(0)
         regroup(0)
@@ -278,11 +279,13 @@ def tile_linearattention_pa_kernel(tc, feature, aspect_v, W, b, out_0, out_1):
         spread_bias()
         regroup_w(4, nc.scalar.copy)
         regroup_w(5, nc.vector.tensor_copy)
+        keep_clock(1)
         transpose(1)
         regroup(1)
         quantise(0, (1, 2))
         regroup_w(6, nc.scalar.copy)
         regroup_w(7, nc.vector.tensor_copy)
+        keep_clock(1)
         multiply(0, 0)
         add_bias(0, 0)
         quantise_w(1)
@@ -296,9 +299,13 @@ def tile_linearattention_pa_kernel(tc, feature, aspect_v, W, b, out_0, out_1):
         transpose(4)
         transpose(5)
 
-        for k in range(PAIRS + BEHIND_CLOSE):
+        closed = 0
+        for k in range(PAIRS + 2):
+            ready = k - BEHIND_CLOSE + 1 if k < PAIRS - 1 else k - 1
+            closing = range(closed, max(ready, 0))
+            closed = max(ready, 0)
             if k + 2 < PAIRS:
-                for n in (1, 0):
+                for n in range(PAIR):
                     regroup(PAIR * (k + 2) + n)
             if 0 < k <= PAIRS:
                 for n in range(PAIR):
@@ -314,9 +321,9 @@ def tile_linearattention_pa_kernel(tc, feature, aspect_v, W, b, out_0, out_1):
                         add_bias(i, h)
                 if n == 1 and k + 2 < PAIRS:
                     quantise(k + 2)
-                if k >= BEHIND_CLOSE:
-                    scale(i - PAIR * BEHIND_CLOSE)
-                    add_to_mean(i - PAIR * BEHIND_CLOSE)
+                for pair in closing:
+                    scale(PAIR * pair + n)
+                    add_to_mean(PAIR * pair + n)
             if k + 3 < PAIRS:
                 for n in range(PAIR):
                     transpose(PAIR * (k + 3) + n)

@@ -67,7 +67,7 @@ def tile_linearattention_pa_kernel(tc, feature, aspect_v, W, b, out_0, out_1):
         nc.vector.memset(ones[:], 1.0)
         bias_row = const.tile([P, M], BF16)
         nc.vector.memset(bias_row[:], 0.0)
-        minus_half = const.tile([P, 1], F32)
+        minus_half = const.tile([P, PAIR], F32)
         nc.vector.memset(minus_half[:], -0.5)
         identity = const.tile([P, P], F32)
         make_identity(nc, identity[:])
@@ -92,8 +92,8 @@ def tile_linearattention_pa_kernel(tc, feature, aspect_v, W, b, out_0, out_1):
         load_w(2, 2)
         load_rows(0)
         nc.sync.dma_start(out=bias_row[0:1, :], in_=b.rearrange("(o m) -> o m", o=1))
-        load_w(4, 2)
         load_rows(1)
+        load_w(4, 2)
         load_w(6, 2)
         for i in range(PAIR, ROW_TILES):
             load_rows(i)
@@ -173,15 +173,11 @@ def tile_linearattention_pa_kernel(tc, feature, aspect_v, W, b, out_0, out_1):
                 in_=pairs_side_by_side(x_bank[i]),
             )
 
-        def quantise(k, tiles=(0, PAIR)):
-            if tiles[0] == 0:
-                codes[k] = mx_pool.tile([P, PAIR * PASSES * P], U32, name="codes", align_bytes=64)
-                scales[k] = mx_pool.tile([P, PAIR * PASSES * P], U8, name="scales", align_bytes=64)
-            cols = slice(tiles[0] * PASSES * P, tiles[1] * PASSES * P)
+        def quantise(k):
+            codes[k] = mx_pool.tile([P, PAIR * PASSES * P], U32, name="codes", align_bytes=64)
+            scales[k] = mx_pool.tile([P, PAIR * PASSES * P], U8, name="scales", align_bytes=64)
             nc.vector.quantize_mx(
-                out=codes[k][:, cols].bitcast(FP8X4),
-                scales=scales[k][:, cols],
-                in_=grouped[k][:, tiles[0] * K : tiles[1] * K],
+                out=codes[k][:].bitcast(FP8X4), scales=scales[k][:], in_=grouped[k][:]
             )
 
         def multiply(i, h):
@@ -211,33 +207,45 @@ def tile_linearattention_pa_kernel(tc, feature, aspect_v, W, b, out_0, out_1):
             factor = 1.0 if ORDER[i][1] == ASPECT else float(TOKENS)
             parts = HALVES if i == ROW_TILES - 1 else 1
             width = M // parts
-            sumsq[i] = norm_pool.tile([P, HALVES], F32, name="sumsq")
+            k, n0 = divmod(i, PAIR)
+            if n0 == 0:
+                sumsq[k] = norm_pool.tile([P, PAIR + 1], F32, name="sumsq")
             squares = scratch_pool.tile([P, M], F32, name="squares")
             for n in range(parts):
                 cols = slice(n * width, (n + 1) * width)
                 nc.scalar.activation(
                     out=squares[:, cols], in_=z[i][:, cols], func=ACT.Square, scale=factor,
-                    accum_out=sumsq[i][:, n : n + 1],
+                    accum_out=sumsq[k][:, n0 + n : n0 + n + 1],
                 )
 
-        def reciprocal_norm(i):
-            floor = 1e-24 if ORDER[i][1] == ASPECT else 1e-24 * TOKENS * TOKENS
-            clamped = norm_pool.tile([P, 1], F32, name="clamped")
-            if i == ROW_TILES - 1:
+        def reciprocal_norms(first, tiles):
+            k, n = divmod(first, PAIR)
+            floors = [1e-24 * (1 if ORDER[i][1] == ASPECT else TOKENS * TOKENS) for i in range(first, first + tiles)]
+            clamped = norm_pool.tile([P, tiles], F32, name="clamped")
+            if first == ROW_TILES - 1:
                 nc.gpsimd.tensor_scalar(
-                    out=clamped[:], in0=sumsq[i][:, 0:1], scalar1=sumsq[i][:, 1:2], scalar2=floor,
-                    op0=ALU.add, op1=ALU.max,
+                    out=clamped[:], in0=sumsq[k][:, n : n + 1], scalar1=sumsq[k][:, n + 1 : n + 2],
+                    scalar2=floors[0], op0=ALU.add, op1=ALU.max,
                 )
+            elif len(set(floors)) == 1:
+                nc.gpsimd.tensor_scalar_max(clamped[:], sumsq[k][:, n : n + tiles], floors[0])
             else:
-                nc.gpsimd.tensor_scalar_max(clamped[:], sumsq[i][:, 0:1], floor)
-            rnorm[i] = norm_pool.tile([P, 1], F32, name="rnorm")
-            nc.gpsimd.tensor_tensor(out=rnorm[i][:], in0=clamped[:], in1=minus_half[:], op=ALU.pow)
+                for j in range(tiles):
+                    nc.gpsimd.tensor_scalar_max(
+                        clamped[:, j : j + 1], sumsq[k][:, n + j : n + j + 1], floors[j]
+                    )
+            inverse = norm_pool.tile([P, tiles], F32, name="inverse")
+            nc.gpsimd.tensor_tensor(
+                out=inverse[:], in0=clamped[:], in1=minus_half[:, 0:tiles], op=ALU.pow
+            )
+            for j in range(tiles):
+                rnorm[first + j] = inverse[:, j : j + 1]
 
         def scale(i):
             g, t = ORDER[i]
             if t == 0:
                 fm[g] = out_pool.tile([P, M], F32, name="fm")
-                nc.scalar.activation(out=fm[g][:], in_=z[i][:], func=ACT.Copy, scale=rnorm[i][:])
+                nc.scalar.activation(out=fm[g][:], in_=z[i][:], func=ACT.Copy, scale=rnorm[i])
             if t == ASPECT:
                 segments = slice(g * P, (g + 1) * P)
                 if i == ROW_TILES - 1:
@@ -245,20 +253,20 @@ def tile_linearattention_pa_kernel(tc, feature, aspect_v, W, b, out_0, out_1):
                         half = slice(h * BANK, (h + 1) * BANK)
                         q = out_pool.tile([P, BANK], F32, name=f"q_half_{h}")
                         if h == 0:
-                            nc.vector.tensor_scalar_mul(q[:], z[i][:, half], rnorm[i][:])
+                            nc.vector.tensor_scalar_mul(q[:], z[i][:, half], rnorm[i])
                         else:
-                            nc.scalar.activation(out=q[:], in_=z[i][:, half], func=ACT.Copy, scale=rnorm[i][:])
+                            nc.scalar.activation(out=q[:], in_=z[i][:, half], func=ACT.Copy, scale=rnorm[i])
                         nc.sync.dma_start(out=out_0[segments, half], in_=q[:])
                 else:
                     q = out_pool.tile([P, M], F32, name="q")
-                    nc.scalar.activation(out=q[:], in_=z[i][:], func=ACT.Copy, scale=rnorm[i][:])
+                    nc.scalar.activation(out=q[:], in_=z[i][:], func=ACT.Copy, scale=rnorm[i])
                     nc.sync.dma_start(out=out_0[segments, :], in_=q[:])
 
         def add_to_mean(i):
             g, t = ORDER[i]
             if 1 <= t < TOKENS:
                 nc.vector.scalar_tensor_tensor(
-                    out=fm[g][:], in0=z[i][:], scalar=rnorm[i][:], in1=fm[g][:],
+                    out=fm[g][:], in0=z[i][:], scalar=rnorm[i], in1=fm[g][:],
                     op0=ALU.mult, op1=ALU.add,
                 )
             if t == TOKENS - 1:
@@ -269,20 +277,19 @@ def tile_linearattention_pa_kernel(tc, feature, aspect_v, W, b, out_0, out_1):
 
         keep_clock(5)
         for t in range(W_TILES // 2):
-            regroup_w(t, nc.scalar.copy if t % 2 == 0 else nc.vector.tensor_copy)
+            regroup_w(t, nc.scalar.copy if t == 0 else nc.vector.tensor_copy)
             if t % 2 == 1:
                 keep_clock(1)
         quantise_w(0)
         transpose(0)
         regroup(0)
-        quantise(0, (0, 1))
-        spread_bias()
-        regroup_w(4, nc.scalar.copy)
-        regroup_w(5, nc.vector.tensor_copy)
-        keep_clock(1)
         transpose(1)
         regroup(1)
-        quantise(0, (1, 2))
+        quantise(0)
+        regroup_w(4, nc.vector.tensor_copy)
+        spread_bias()
+        regroup_w(5, nc.vector.tensor_copy)
+        keep_clock(1)
         regroup_w(6, nc.scalar.copy)
         regroup_w(7, nc.vector.tensor_copy)
         keep_clock(1)
@@ -310,14 +317,17 @@ def tile_linearattention_pa_kernel(tc, feature, aspect_v, W, b, out_0, out_1):
             if 0 < k <= PAIRS:
                 for n in range(PAIR):
                     sum_of_squares(PAIR * (k - 1) + n)
-                    reciprocal_norm(PAIR * (k - 1) + n)
+                    if k == PAIRS:
+                        reciprocal_norms(PAIR * (k - 1) + n, 1)
+                if k < PAIRS:
+                    reciprocal_norms(PAIR * (k - 1), PAIR)
             for n in range(PAIR):
                 i = PAIR * k + n
                 if k < PAIRS:
                     halves = [h for h in range(HALVES) if k > 0 or h > 0]
                     for h in halves:
                         multiply(i, h)
-                    for h in reversed(halves):
+                    for h in halves if i == ROW_TILES - 1 else reversed(halves):
                         add_bias(i, h)
                 if n == 1 and k + 2 < PAIRS:
                     quantise(k + 2)
@@ -327,3 +337,4 @@ def tile_linearattention_pa_kernel(tc, feature, aspect_v, W, b, out_0, out_1):
             if k + 3 < PAIRS:
                 for n in range(PAIR):
                     transpose(PAIR * (k + 3) + n)
+                keep_clock(2)

@@ -153,6 +153,7 @@ def tile_linearattention_pa_kernel(tc, feature, aspect_v, W, b, out_0, out_1):
         codes = {}
         scales = {}
         y_bank = {}
+        sum_bank = {}
         z = {}
         sumsq = {}
         rnorm = {}
@@ -243,7 +244,7 @@ def tile_linearattention_pa_kernel(tc, feature, aspect_v, W, b, out_0, out_1):
 
         def scale(i):
             g, t = ORDER[i]
-            if t == 0:
+            if t == 0 and g < GROUPS - 1:
                 fm[g] = out_pool.tile([P, M], F32, name="fm")
                 nc.scalar.activation(out=fm[g][:], in_=z[i][:], func=ACT.Copy, scale=rnorm[i])
             if t == ASPECT:
@@ -262,8 +263,43 @@ def tile_linearattention_pa_kernel(tc, feature, aspect_v, W, b, out_0, out_1):
                     nc.scalar.activation(out=q[:], in_=z[i][:], func=ACT.Copy, scale=rnorm[i])
                     nc.sync.dma_start(out=out_0[segments, :], in_=q[:])
 
+        def diagonal(i):
+            square = norm_pool.tile([P, P], F32, name="square")
+            nc.scalar.activation(out=square[:], in_=identity[:], func=ACT.Copy, scale=rnorm[i])
+            return square
+
+        def add_on_tensor(squares):
+            for h in range(HALVES):
+                sum_bank[h] = psum_t.tile([P, BANK], F32, name="xt")
+                for n, (i, square) in enumerate(squares.items()):
+                    nc.tensor.matmul(
+                        out=sum_bank[h][:],
+                        lhsT=square[:],
+                        rhs=z[i][:, h * BANK : (h + 1) * BANK],
+                        start=(n == 0),
+                        stop=(n == len(squares) - 1),
+                    )
+
+        def finish_last_mean(i, j):
+            fm_last = out_pool.tile([P, M], F32, name="fm")
+            for h in range(HALVES):
+                half = slice(h * BANK, (h + 1) * BANK)
+                nc.vector.scalar_tensor_tensor(
+                    out=fm_last[:, half], in0=z[i][:, half], scalar=rnorm[i], in1=sum_bank[h][:],
+                    op0=ALU.mult, op1=ALU.add,
+                )
+                nc.vector.scalar_tensor_tensor(
+                    out=fm_last[:, half], in0=z[j][:, half], scalar=rnorm[j], in1=fm_last[:, half],
+                    op0=ALU.mult, op1=ALU.add,
+                )
+                nc.sync.dma_start(out=out_1[(GROUPS - 1) * P :, half], in_=fm_last[:, half])
+
         def add_to_mean(i):
             g, t = ORDER[i]
+            if g == GROUPS - 1:
+                if t == TOKENS - 1:
+                    finish_last_mean(i - 1, i)
+                return
             if 1 <= t < TOKENS:
                 nc.vector.scalar_tensor_tensor(
                     out=fm[g][:], in0=z[i][:], scalar=rnorm[i], in1=fm[g][:],
@@ -317,8 +353,14 @@ def tile_linearattention_pa_kernel(tc, feature, aspect_v, W, b, out_0, out_1):
             if 0 < k <= PAIRS:
                 for n in range(PAIR):
                     sum_of_squares(PAIR * (k - 1) + n)
+                    if k == PAIRS - 1 and n == 0:
+                        early_tokens = [ORDER.index((GROUPS - 1, t)) for t in (0, 1)]
+                        squares = {i: diagonal(i) for i in early_tokens}
                     if k == PAIRS:
                         reciprocal_norms(PAIR * (k - 1) + n, 1)
+                    else:
+                        for pair in closing:
+                            scale(PAIR * pair + n)
                 if k < PAIRS:
                     reciprocal_norms(PAIR * (k - 1), PAIR)
             for n in range(PAIR):
@@ -332,8 +374,11 @@ def tile_linearattention_pa_kernel(tc, feature, aspect_v, W, b, out_0, out_1):
                 if n == 1 and k + 2 < PAIRS:
                     quantise(k + 2)
                 for pair in closing:
-                    scale(PAIR * pair + n)
+                    if k >= PAIRS:
+                        scale(PAIR * pair + n)
                     add_to_mean(PAIR * pair + n)
+            if k == PAIRS - 1:
+                add_on_tensor(squares)
             if k + 3 < PAIRS:
                 for n in range(PAIR):
                     transpose(PAIR * (k + 3) + n)

@@ -252,11 +252,8 @@ def tile_linearattention_pa_kernel(tc, feature, aspect_v, W, b, out_0, out_1):
                 if i == ROW_TILES - 1:
                     for h in range(HALVES):
                         half = slice(h * BANK, (h + 1) * BANK)
-                        q = out_pool.tile([P, BANK], F32, name=f"q_half_{h}")
-                        if h == 0:
-                            nc.vector.tensor_scalar_mul(q[:], z[i][:, half], rnorm[i])
-                        else:
-                            nc.scalar.activation(out=q[:], in_=z[i][:, half], func=ACT.Copy, scale=rnorm[i])
+                        q = out_pool.tile([P, BANK], F32, name="q_half")
+                        nc.scalar.activation(out=q[:], in_=z[i][:, half], func=ACT.Copy, scale=rnorm[i])
                         nc.sync.dma_start(out=out_0[segments, half], in_=q[:])
                 else:
                     q = out_pool.tile([P, M], F32, name="q")
@@ -373,13 +370,16 @@ def tile_linearattention_pa_kernel(tc, feature, aspect_v, W, b, out_0, out_1):
                         add_bias(i, h)
                 if n == 1 and k + 2 < PAIRS:
                     quantise(k + 2)
-                for pair in closing:
-                    if k >= PAIRS:
-                        scale(PAIR * pair + n)
-                    add_to_mean(PAIR * pair + n)
+                if k != PAIRS - 1:
+                    for pair in closing:
+                        if k >= PAIRS:
+                            scale(PAIR * pair + n)
+                        add_to_mean(PAIR * pair + n)
             if k == PAIRS - 1:
                 add_on_tensor(squares)
+                for pair in closing:
+                    for n in range(PAIR):
+                        add_to_mean(PAIR * pair + n)
             if k + 3 < PAIRS:
                 for n in range(PAIR):
                     transpose(PAIR * (k + 3) + n)
-                keep_clock(2)

@@ -59,9 +59,8 @@ def tile_linearattention_pa_kernel(tc, feature, aspect_v, W, b, out_0, out_1):
         scratch_pool = stack.enter_context(tc.tile_pool(name="scratch", bufs=8))
         norm_pool = stack.enter_context(tc.tile_pool(name="norm", bufs=9))
         out_pool = stack.enter_context(tc.tile_pool(name="out", bufs=2))
-        psum_t = stack.enter_context(tc.psum_pool(name="psum_t", bufs=2))
+        psum_t = stack.enter_context(tc.psum_pool(name="psum_t", bufs=3))
         psum_y = stack.enter_context(tc.psum_pool(name="psum_y", bufs=5))
-        psum_idle = stack.enter_context(tc.psum_pool(name="psum_idle", bufs=1))
 
         ones = const.tile([P, BANK], BF16)
         nc.vector.memset(ones[:], 1.0)
@@ -98,9 +97,8 @@ def tile_linearattention_pa_kernel(tc, feature, aspect_v, W, b, out_0, out_1):
         for i in range(PAIR, ROW_TILES):
             load_rows(i)
 
-        idle_bank = psum_idle.tile([P, BANK], F32)
-
         def keep_clock(passes):
+            idle_bank = psum_y.tile([P, BANK], F32, name="y")
             for n in range(passes):
                 nc.tensor.matmul(out=idle_bank[:], lhsT=ones[:, 0:P], rhs=ones[:], start=True, stop=True)
 
@@ -329,10 +327,10 @@ def tile_linearattention_pa_kernel(tc, feature, aspect_v, W, b, out_0, out_1):
         multiply(0, 0)
         add_bias(0, 0)
         quantise_w(1)
-        multiply(1, 0)
-        add_bias(1, 0)
         transpose(2)
         transpose(3)
+        multiply(1, 0)
+        add_bias(1, 0)
         regroup(2)
         regroup(3)
         quantise(1)

from contextlib import ExitStack

import concourse.mybir as mybir
from concourse.masks import make_identity

F32 = mybir.dt.float32
BF16 = mybir.dt.bfloat16
U32 = mybir.dt.uint32
U8 = mybir.dt.uint8
FP8X4 = mybir.dt.float8_e4m3fn_x4
ALU = mybir.AluOpType
ACT = mybir.ActivationFunctionType

P = 128
SEGMENTS = 1024
TOKENS = 4
K = 1024
M = 1024
K_PASS = 4 * P
PASSES = K // K_PASS
WORDS = K // 2
BANK = 512
HALVES = M // BANK
GROUPS = SEGMENTS // P
TILES_PER_GROUP = TOKENS + 1
ROW_TILES = GROUPS * TILES_PER_GROUP
ASPECT = TOKENS
ASPECT_LAG = 1


def row_tile_order():
    order = []
    for g in range(GROUPS + ASPECT_LAG):
        if g < GROUPS:
            order += [(g, t) for t in range(TOKENS)]
        if g >= ASPECT_LAG:
            order += [(g - ASPECT_LAG, ASPECT)]
    return order


ORDER = row_tile_order()
W_TILES = M // P

PAIR = 2
PAIRS = ROW_TILES // PAIR
BEHIND_CLOSE = 3

FLOPS = 2 * (SEGMENTS * TOKENS + SEGMENTS) * K * M


def tile_linearattention_pa_kernel(tc, feature, aspect_v, W, b, out_0, out_1):
    nc = tc.nc
    with ExitStack() as stack:
        const = stack.enter_context(tc.tile_pool(name="const", bufs=1))
        raw_pool = stack.enter_context(tc.tile_pool(name="raw", bufs=28))
        grouped_pool = stack.enter_context(tc.tile_pool(name="grouped", bufs=3))
        mx_pool = stack.enter_context(tc.tile_pool(name="mx", bufs=4))
        z_pool = stack.enter_context(tc.tile_pool(name="z", bufs=12))
        scratch_pool = stack.enter_context(tc.tile_pool(name="scratch", bufs=8))
        norm_pool = stack.enter_context(tc.tile_pool(name="norm", bufs=9))
        out_pool = stack.enter_context(tc.tile_pool(name="out", bufs=2))
        psum_t = stack.enter_context(tc.psum_pool(name="psum_t", bufs=3))
        psum_y = stack.enter_context(tc.psum_pool(name="psum_y", bufs=5))

        ones = const.tile([P, BANK], BF16)
        nc.vector.memset(ones[:], 1.0)
        bias_row = const.tile([P, M], BF16)
        nc.vector.memset(bias_row[:], 0.0)
        minus_half = const.tile([P, PAIR], F32)
        nc.vector.memset(minus_half[:], -0.5)
        identity = const.tile([P, P], F32)
        make_identity(nc, identity[:])

        w_raw = const.tile([P, W_TILES * K], BF16)
        w_raw_tiles = w_raw[:].rearrange("p (t k) -> p t k", k=K)
        w_rows = W.rearrange("(t p) k -> p t k", p=P)
        raw = {}

        def load_w(t, tiles):
            nc.sync.dma_start(out=w_raw_tiles[:, t : t + tiles, :], in_=w_rows[:, t : t + tiles, :])

        def load_rows(i):
            g, t = ORDER[i]
            segments = slice(g * P, (g + 1) * P)
            rows = aspect_v[segments, :] if t == ASPECT else feature[segments, t, :]
            raw[i] = raw_pool.tile([P, K], BF16, name="raw")
            nc.sync.dma_start(out=raw[i][:], in_=rows)

        load_w(0, 1)
        load_w(1, 1)
        load_w(2, 2)
        load_rows(0)
        nc.sync.dma_start(out=bias_row[0:1, :], in_=b.rearrange("(o m) -> o m", o=1))
        load_rows(1)
        load_w(4, 2)
        load_w(6, 2)
        for i in range(PAIR, ROW_TILES):
            load_rows(i)

        def keep_clock(passes):
            idle_bank = psum_y.tile([P, BANK], F32, name="y")
            for n in range(passes):
                nc.tensor.matmul(out=idle_bank[:], lhsT=ones[:, 0:P], rhs=ones[:], start=True, stop=True)

        def transpose_rows(words, bank):
            for c in range(PASSES):
                for u in range(2):
                    j = 2 * c + u
                    nc.tensor.transpose(
                        bank[:, j * P : (j + 1) * P],
                        words[:, c * 2 * P + u : (c + 1) * 2 * P : 2],
                        identity[:],
                    )

        def pairs_side_by_side(bank):
            return bank.rearrange("p (c u r) -> p c r u", c=PASSES, u=2)

        bias = const.tile([P, M], BF16)

        def spread_bias():
            b_bank = psum_y.tile([P, M], BF16, name="y")
            for h in range(HALVES):
                half = slice(h * BANK, (h + 1) * BANK)
                nc.tensor.matmul(out=b_bank[:, half], lhsT=ones[:, 0:P], rhs=bias_row[:, half], start=True, stop=True)
            nc.scalar.copy(out=bias[:], in_=b_bank[:])

        w_grouped = const.tile([P, PASSES * M * 4], BF16, align_bytes=64)
        w_grouped_words = w_grouped[:].bitcast(F32).rearrange(
            "p (c m u) -> p c m u", c=PASSES, u=2
        )
        w_codes = const.tile([P, PASSES * M], U32, align_bytes=64)
        w_scales = const.tile([P, PASSES * M], U8, align_bytes=64)
        w_words = w_raw[:].bitcast(F32)

        def regroup_w(t, copy):
            w_bank = psum_y.tile([P, BANK], F32, name="y")
            transpose_rows(w_words[:, t * WORDS : (t + 1) * WORDS], w_bank)
            copy(out=w_grouped_words[:, :, t * P : (t + 1) * P, :], in_=pairs_side_by_side(w_bank))

        def quantise_w(h):
            for c in range(PASSES):
                lo = c * M + h * BANK
                nc.vector.quantize_mx(
                    out=w_codes[:, lo : lo + BANK].bitcast(FP8X4),
                    scales=w_scales[:, lo : lo + BANK],
                    in_=w_grouped[:, 4 * lo : 4 * (lo + BANK)],
                )

        x_bank = {}
        grouped = {}
        codes = {}
        scales = {}
        y_bank = {}
        sum_bank = {}
        z = {}
        sumsq = {}
        rnorm = {}
        fm = {}

        def transpose(i):
            x_bank[i] = psum_t.tile([P, BANK], F32, name="xt")
            transpose_rows(raw[i][:].bitcast(F32), x_bank[i])

        def regroup(i):
            k, n = divmod(i, PAIR)
            if k not in grouped:
                grouped[k] = grouped_pool.tile([P, PAIR * K], BF16, name="grouped", align_bytes=64)
            nc.scalar.copy(
                out=grouped[k][:, n * K : (n + 1) * K]
                .bitcast(F32)
                .rearrange("p (c r u) -> p c r u", c=PASSES, u=2),
                in_=pairs_side_by_side(x_bank[i]),
            )

        def quantise(k):
            codes[k] = mx_pool.tile([P, PAIR * PASSES * P], U32, name="codes", align_bytes=64)
            scales[k] = mx_pool.tile([P, PAIR * PASSES * P], U8, name="scales", align_bytes=64)
            nc.vector.quantize_mx(
                out=codes[k][:].bitcast(FP8X4), scales=scales[k][:], in_=grouped[k][:]
            )

        def multiply(i, h):
            k, n = divmod(i, PAIR)
            y = psum_y.tile([P, BANK], F32, name="y")
            for c in range(PASSES):
                rows = slice((n * PASSES + c) * P, (n * PASSES + c + 1) * P)
                cols = slice(c * M + h * BANK, c * M + (h + 1) * BANK)
                nc.tensor.matmul_mx(
                    out=y[:],
                    lhsT=codes[k][:, rows].bitcast(FP8X4),
                    lhsT_scale=scales[k][:, rows],
                    rhs=w_codes[:, cols].bitcast(FP8X4),
                    rhs_scale=w_scales[:, cols],
                    start=(c == 0),
                    stop=(c == PASSES - 1),
                )
            y_bank[i, h] = y

        def add_bias(i, h):
            if i not in z:
                z[i] = z_pool.tile([P, M], F32, name="z")
            half = slice(h * BANK, (h + 1) * BANK)
            nc.vector.tensor_tensor(out=z[i][:, half], in0=y_bank[i, h][:], in1=bias[:, half], op=ALU.add)

        def sum_of_squares(i):
            factor = 1.0 if ORDER[i][1] == ASPECT else float(TOKENS)
            parts = HALVES if i == ROW_TILES - 1 else 1
            width = M // parts
            k, n0 = divmod(i, PAIR)
            if n0 == 0:
                sumsq[k] = norm_pool.tile([P, PAIR + 1], F32, name="sumsq")
            squares = scratch_pool.tile([P, M], F32, name="squares")
            for n in range(parts):
                cols = slice(n * width, (n + 1) * width)
                nc.scalar.activation(
                    out=squares[:, cols], in_=z[i][:, cols], func=ACT.Square, scale=factor,
                    accum_out=sumsq[k][:, n0 + n : n0 + n + 1],
                )

        def reciprocal_norms(first, tiles):
            k, n = divmod(first, PAIR)
            floors = [1e-24 * (1 if ORDER[i][1] == ASPECT else TOKENS * TOKENS) for i in range(first, first + tiles)]
            clamped = norm_pool.tile([P, tiles], F32, name="clamped")
            if first == ROW_TILES - 1:
                nc.gpsimd.tensor_scalar(
                    out=clamped[:], in0=sumsq[k][:, n : n + 1], scalar1=sumsq[k][:, n + 1 : n + 2],
                    scalar2=floors[0], op0=ALU.add, op1=ALU.max,
                )
            elif len(set(floors)) == 1:
                nc.gpsimd.tensor_scalar_max(clamped[:], sumsq[k][:, n : n + tiles], floors[0])
            else:
                for j in range(tiles):
                    nc.gpsimd.tensor_scalar_max(
                        clamped[:, j : j + 1], sumsq[k][:, n + j : n + j + 1], floors[j]
                    )
            inverse = norm_pool.tile([P, tiles], F32, name="inverse")
            nc.gpsimd.tensor_tensor(
                out=inverse[:], in0=clamped[:], in1=minus_half[:, 0:tiles], op=ALU.pow
            )
            for j in range(tiles):
                rnorm[first + j] = inverse[:, j : j + 1]

        def scale(i):
            g, t = ORDER[i]
            if t == 0 and g < GROUPS - 1:
                fm[g] = out_pool.tile([P, M], F32, name="fm")
                nc.scalar.activation(out=fm[g][:], in_=z[i][:], func=ACT.Copy, scale=rnorm[i])
            if t == ASPECT:
                segments = slice(g * P, (g + 1) * P)
                if i == ROW_TILES - 1:
                    for h in range(HALVES):
                        half = slice(h * BANK, (h + 1) * BANK)
                        q = out_pool.tile([P, BANK], F32, name="q_half")
                        nc.scalar.activation(out=q[:], in_=z[i][:, half], func=ACT.Copy, scale=rnorm[i])
                        nc.sync.dma_start(out=out_0[segments, half], in_=q[:])
                else:
                    q = out_pool.tile([P, M], F32, name="q")
                    nc.scalar.activation(out=q[:], in_=z[i][:], func=ACT.Copy, scale=rnorm[i])
                    nc.sync.dma_start(out=out_0[segments, :], in_=q[:])

        def diagonal(i):
            square = norm_pool.tile([P, P], F32, name="square")
            nc.scalar.activation(out=square[:], in_=identity[:], func=ACT.Copy, scale=rnorm[i])
            return square

        def add_on_tensor(squares):
            for h in range(HALVES):
                sum_bank[h] = psum_t.tile([P, BANK], F32, name="xt")
                for n, (i, square) in enumerate(squares.items()):
                    nc.tensor.matmul(
                        out=sum_bank[h][:],
                        lhsT=square[:],
                        rhs=z[i][:, h * BANK : (h + 1) * BANK],
                        start=(n == 0),
                        stop=(n == len(squares) - 1),
                    )

        def finish_last_mean(i, j):
            fm_last = out_pool.tile([P, M], F32, name="fm")
            for h in range(HALVES):
                half = slice(h * BANK, (h + 1) * BANK)
                nc.vector.scalar_tensor_tensor(
                    out=fm_last[:, half], in0=z[i][:, half], scalar=rnorm[i], in1=sum_bank[h][:],
                    op0=ALU.mult, op1=ALU.add,
                )
                nc.vector.scalar_tensor_tensor(
                    out=fm_last[:, half], in0=z[j][:, half], scalar=rnorm[j], in1=fm_last[:, half],
                    op0=ALU.mult, op1=ALU.add,
                )
                nc.sync.dma_start(out=out_1[(GROUPS - 1) * P :, half], in_=fm_last[:, half])

        def add_to_mean(i):
            g, t = ORDER[i]
            if g == GROUPS - 1:
                if t == TOKENS - 1:
                    finish_last_mean(i - 1, i)
                return
            if 1 <= t < TOKENS:
                nc.vector.scalar_tensor_tensor(
                    out=fm[g][:], in0=z[i][:], scalar=rnorm[i], in1=fm[g][:],
                    op0=ALU.mult, op1=ALU.add,
                )
            if t == TOKENS - 1:
                nc.sync.dma_start(out=out_1[g * P : (g + 1) * P, :], in_=fm[g][:])

        engines = {mybir.EngineType.PE, mybir.EngineType.DVE, mybir.EngineType.Activation}
        stack.enter_context(tc.manual_schedule(engines=engines))

        keep_clock(5)
        for t in range(W_TILES // 2):
            regroup_w(t, nc.scalar.copy if t == 0 else nc.vector.tensor_copy)
            if t % 2 == 1:
                keep_clock(1)
        quantise_w(0)
        transpose(0)
        regroup(0)
        transpose(1)
        regroup(1)
        quantise(0)
        regroup_w(4, nc.vector.tensor_copy)
        spread_bias()
        regroup_w(5, nc.vector.tensor_copy)
        keep_clock(1)
        regroup_w(6, nc.scalar.copy)
        regroup_w(7, nc.vector.tensor_copy)
        keep_clock(1)
        multiply(0, 0)
        add_bias(0, 0)
        quantise_w(1)
        transpose(2)
        transpose(3)
        multiply(1, 0)
        add_bias(1, 0)
        regroup(2)
        regroup(3)
        quantise(1)
        transpose(4)
        transpose(5)

        closed = 0
        for k in range(PAIRS + 2):
            ready = k - BEHIND_CLOSE + 1 if k < PAIRS - 1 else k - 1
            closing = range(closed, max(ready, 0))
            closed = max(ready, 0)
            if k + 2 < PAIRS:
                for n in range(PAIR):
                    regroup(PAIR * (k + 2) + n)
            if 0 < k <= PAIRS:
                for n in range(PAIR):
                    sum_of_squares(PAIR * (k - 1) + n)
                    if k == PAIRS - 1 and n == 0:
                        early_tokens = [ORDER.index((GROUPS - 1, t)) for t in (0, 1)]
                        squares = {i: diagonal(i) for i in early_tokens}
                    if k == PAIRS:
                        reciprocal_norms(PAIR * (k - 1) + n, 1)
                    else:
                        for pair in closing:
                            scale(PAIR * pair + n)
                if k < PAIRS:
                    reciprocal_norms(PAIR * (k - 1), PAIR)
            for n in range(PAIR):
                i = PAIR * k + n
                if k < PAIRS:
                    halves = [h for h in range(HALVES) if k > 0 or h > 0]
                    for h in halves:
                        multiply(i, h)
                    for h in halves if i == ROW_TILES - 1 else reversed(halves):
                        add_bias(i, h)
                if n == 1 and k + 2 < PAIRS:
                    quantise(k + 2)
                if k != PAIRS - 1:
                    for pair in closing:
                        if k >= PAIRS:
                            scale(PAIR * pair + n)
                        add_to_mean(PAIR * pair + n)
            if k == PAIRS - 1:
                add_on_tensor(squares)
                for pair in closing:
                    for n in range(PAIR):
                        add_to_mean(PAIR * pair + n)
            if k + 3 < PAIRS:
                for n in range(PAIR):
                    transpose(PAIR * (k + 3) + n)
